import numpy as np
import ml_dtypes


def mxq(x, axis, fmt="e4m3"):
    dtype, down = {"e4m3": (ml_dtypes.float8_e4m3fn, 7), "e5m2": (ml_dtypes.float8_e5m2, 14)}[fmt]
    v = np.moveaxis(np.asarray(x, np.float32).astype(ml_dtypes.bfloat16).astype(np.float64), axis, -1)
    blocks = v.reshape(v.shape[:-1] + (-1, 32))
    amax = np.abs(blocks).max(-1, keepdims=True)
    byte = np.maximum(np.where(amax > 0, np.frexp(amax)[1] - 1 + 127, 0) - down, 1)
    scale = np.exp2(byte - 127.0)
    codes = (blocks / scale).astype(np.float32).astype(dtype).astype(np.float64)
    return np.moveaxis((codes * scale).reshape(v.shape), -1, axis)


WIDE = False


def mx_kscale(k):
    if not WIDE:
        return np.ones(k)
    levels = np.array([10, -10, 5, -5, 0])
    a = np.random.permutation(np.resize(levels, k // 512 * 4)).reshape(k // 512, 4)
    idx = np.arange(k)
    return np.exp2(a[idx // 512, idx % 128 // 32])


BF16 = ml_dtypes.bfloat16


def bf(x):
    return np.asarray(x, np.float32).astype(BF16)


def f64(x):
    return np.asarray(x).astype(np.float64)


B, IN, H, OUT, L, STEPS = 1024, 512, 1024, 128, 3, 3
LN_EPS = 1e-5


def layer_norm(v, g, b):
    m = v.mean(-1, keepdims=True)
    var = ((v - m) ** 2).mean(-1, keepdims=True)
    return (v - m) / np.sqrt(var + LN_EPS) * g + b


def setup_inputs():
    s = mx_kscale(H)
    s = s / s.max()
    return {"h": bf(np.random.standard_normal((B, H)) * s),
            "W_liq": bf(np.random.standard_normal((L, H, H)) / np.sqrt(H) / s),
            "b_liq": bf(np.random.standard_normal((L, H)) * 0.3),
            "g_liq": bf(1.0 + 0.1 * np.random.standard_normal((L, H))),
            "beta_liq": bf(np.random.standard_normal((L, H)) * 0.3)}


def reference(h, W_liq, b_liq, g_liq, beta_liq):
    h = f64(h)
    lin = mxq(h, 1, "e4m3") @ mxq(f64(W_liq), 2, "e4m3").transpose(0, 2, 1)
    pre = h[None] + lin + f64(b_liq)[:, None, :]
    return layer_norm(pre, f64(g_liq)[:, None, :], f64(beta_liq)[:, None, :]).sum(0)

@@ -1,0 +1,183 @@
+from contextlib import ExitStack
+
+import concourse.mybir as mybir
+from concourse.masks import make_identity
+
+F32 = mybir.dt.float32
+BF16 = mybir.dt.bfloat16
+U32 = mybir.dt.uint32
+U8 = mybir.dt.uint8
+I32 = mybir.dt.int32
+FP8X4 = mybir.dt.float8_e4m3fn_x4
+ADD = mybir.AluOpType.add
+MULT = mybir.AluOpType.mult
+ACT = mybir.ActivationFunctionType
+
+P = 128
+B = 1024
+H = 1024
+L = 3
+LN_EPS = 1e-5
+PACK = 4
+K_PASS = P * PACK
+PASSES = H // K_PASS
+BANK = 512
+HALVES = H // BANK
+UNIT_TILES = 4
+UNIT_ROWS = UNIT_TILES * P
+UNITS = B // UNIT_ROWS
+
+FLOPS = 2 * L * B * H * H
+
+
+def tile_advancedliquidneuralnetwork_pa_kernel(tc, h, W_liq, b_liq, g_liq, beta_liq, out):
+    nc = tc.nc
+    with ExitStack() as ctx:
+        const = ctx.enter_context(tc.tile_pool(name="const", bufs=1))
+        raw_pool = ctx.enter_context(tc.tile_pool(name="raw", bufs=1))
+        stage = ctx.enter_context(tc.tile_pool(name="stage", bufs=3))
+        keep = ctx.enter_context(tc.tile_pool(name="keep", bufs=1))
+        work = ctx.enter_context(tc.tile_pool(name="work", bufs=4))
+        acc_pool = ctx.enter_context(tc.tile_pool(name="acc", bufs=6))
+        stats = ctx.enter_context(tc.tile_pool(name="stats", bufs=8))
+        psum = ctx.enter_context(tc.psum_pool(name="psum", bufs=4))
+
+        rows = const.tile([P, H], BF16)
+        nc.vector.memset(rows[:].bitcast(I32), 0)
+        nc.scalar.dma_start(out=rows[0:L, :], in_=b_liq)
+        nc.scalar.dma_start(out=rows[L : 2 * L, :], in_=g_liq)
+        nc.scalar.dma_start(out=rows[2 * L : 3 * L, :], in_=beta_liq)
+
+        def load_unit(name, dram_rows):
+            raw = raw_pool.tile([P, UNIT_TILES, H], BF16, name=name)
+            nc.sync.dma_start(out=raw[:], in_=dram_rows.rearrange("(j p) k -> p j k", p=P))
+            return raw
+
+        def unit_rows(u):
+            return slice(u * UNIT_ROWS, (u + 1) * UNIT_ROWS)
+
+        h_raw = [None] * UNITS
+        w_raw = {}
+        h_raw[0] = load_unit("h_raw0", h[unit_rows(0), :])
+        for l in range(L):
+            for u in range(UNITS):
+                w_raw[(l, u)] = load_unit("w_raw%d_%d" % (l, u), W_liq[l, unit_rows(u), :])
+        h_raw[1] = load_unit("h_raw1", h[unit_rows(1), :])
+
+        ident_f32 = const.tile([P, P], F32)
+        make_identity(nc, ident_f32[:])
+        ident_bf16 = const.tile([P, P], BF16)
+        make_identity(nc, ident_bf16[:])
+        eps = const.tile([P, 1], F32)
+        nc.vector.memset(eps[:], LN_EPS)
+        warm = const.tile([P, 1], F32)
+        nc.scalar.activation(out=warm[:], in_=eps[:], func=ACT.Sqrt)
+
+        def spread_rows(dest, picked):
+            for half in range(HALVES):
+                cols = slice(half * BANK, (half + 1) * BANK)
+                spread = psum.tile([P, BANK], F32, tag="t")
+                for r in picked:
+                    nc.tensor.matmul(
+                        out=spread[:],
+                        lhsT=ident_bf16[:, r : r + 1].to_broadcast([P, P]),
+                        rhs=rows[:, cols],
+                        start=(r == picked[0]),
+                        stop=(r == picked[-1]),
+                    )
+                nc.scalar.copy(out=dest[:, cols], in_=spread[:])
+
+        bias_bc = const.tile([P, L, H], BF16)
+        gain_bc = const.tile([P, L, H], BF16)
+        shift_bc = const.tile([P, H], F32)
+        for l in range(L):
+            spread_rows(bias_bc[:, l, :], [l])
+        for l in range(L):
+            spread_rows(gain_bc[:, l, :], [L + l])
+        spread_rows(shift_bc, [2 * L + l for l in range(L)])
+
+        h_codes = keep.tile([P, PASSES, B], U32, align_bytes=64)
+        h_scales = keep.tile([P, PASSES, B], U8, align_bytes=64)
+        w_codes = keep.tile([P, L, PASSES, H], U32, align_bytes=64)
+        w_scales = keep.tile([P, L, PASSES, H], U8, align_bytes=64)
+
+        def quantise_unit(raw, codes, scales):
+            grouped = stage.tile([P, PASSES, UNIT_TILES, P, PACK], BF16, align_bytes=64)
+            grouped_words = grouped[:].bitcast(F32)
+            for j in range(UNIT_TILES):
+                raw_words = raw[:, j, :].bitcast(F32)
+                flipped = psum.tile([P, PASSES, 2, P], F32, tag="t")
+                for c in range(PASSES):
+                    for u in range(2):
+                        first = (2 * c + u) * P
+                        nc.tensor.transpose(flipped[:, c, u, :], raw_words[:, first : first + P], ident_f32[:])
+                nc.scalar.copy(out=grouped_words[:, :, j, :, :], in_=flipped[:].rearrange("p c u r -> p c r u"))
+            for c in range(PASSES):
+                nc.vector.quantize_mx(
+                    out=codes[:, c, :].bitcast(FP8X4),
+                    scales=scales[:, c, :],
+                    in_=grouped[:, c].rearrange("p j r t -> p (j r t)"),
+                )
+
+        def quantise_h(u):
+            quantise_unit(h_raw[u], h_codes[:, :, unit_rows(u)], h_scales[:, :, unit_rows(u)])
+
+        def quantise_w(l):
+            for u in range(UNITS):
+                quantise_unit(w_raw[(l, u)], w_codes[:, l, :, unit_rows(u)], w_scales[:, l, :, unit_rows(u)])
+
+        def branch(l, u, j, acc):
+            tile_cols = slice((u * UNIT_TILES + j) * P, (u * UNIT_TILES + j + 1) * P)
+            resid = work.tile([P, H], F32)
+            nc.gpsimd.tensor_tensor(out=resid[:], in0=h_raw[u][:, j, :], in1=bias_bc[:, l, :], op=ADD)
+            pre = work.tile([P, H], F32)
+            row_sum = stats.tile([P, HALVES], F32)
+            for half in range(HALVES):
+                cols = slice(half * BANK, (half + 1) * BANK)
+                product = psum.tile([P, BANK], F32, tag="x")
+                for c in range(PASSES):
+                    nc.tensor.matmul_mx(
+                        out=product[:],
+                        lhsT=h_codes[:, c, tile_cols].bitcast(FP8X4),
+                        lhsT_scale=h_scales[:, c, tile_cols],
+                        rhs=w_codes[:, l, c, cols].bitcast(FP8X4),
+                        rhs_scale=w_scales[:, l, c, cols],
+                        start=(c == 0),
+                        stop=(c == PASSES - 1),
+                    )
+                nc.vector.scalar_tensor_tensor(
+                    out=pre[:, cols], in0=product[:], scalar=0.0, in1=resid[:, cols],
+                    op0=ADD, op1=ADD, accum_out=row_sum[:, half : half + 1],
+                )
+            neg_mean = stats.tile([P, 1], F32)
+            nc.vector.tensor_scalar(
+                out=neg_mean[:], in0=row_sum[:, 0:1], scalar1=row_sum[:, 1:2], scalar2=-1.0 / H, op0=ADD, op1=MULT
+            )
+            squares = work.tile([P, H], F32, bufs=2)
+            sum_sq = stats.tile([P, 1], F32)
+            nc.scalar.activation(out=squares[:], in_=pre[:], func=ACT.Square, bias=neg_mean[:], scale=1.0, accum_out=sum_sq[:])
+            std = stats.tile([P, 1], F32)
+            nc.scalar.activation(out=std[:], in_=sum_sq[:], func=ACT.Sqrt, bias=eps[:], scale=1.0 / H)
+            rstd = stats.tile([P, 1], F32)
+            nc.vector.reciprocal(rstd[:], std[:])
+            nc.vector.scalar_tensor_tensor(
+                out=pre[:], in0=pre[:], scalar=neg_mean[:], in1=gain_bc[:, l, :], op0=ADD, op1=MULT
+            )
+            nc.vector.scalar_tensor_tensor(
+                out=acc[:], in0=pre[:], scalar=rstd[:], in1=(shift_bc[:] if l == 0 else acc[:]), op0=MULT, op1=ADD
+            )
+
+        quantise_h(0)
+        quantise_w(0)
+        for u in range(UNITS):
+            accs = [acc_pool.tile([P, H], F32, name="acc") for j in range(UNIT_TILES)]
+            for l in range(L):
+                if u == 0 and l + 1 < L:
+                    quantise_w(l + 1)
+                if u + 1 < UNITS and l == L - 1:
+                    quantise_h(u + 1)
+                for j in range(UNIT_TILES):
+                    branch(l, u, j, accs[j])
+            for j in range(UNIT_TILES):
+                first = (u * UNIT_TILES + j) * P
+                nc.sync.dma_start(out=out[first : first + P, :], in_=accs[j][:])

@@ -26,6 +26,8 @@ HALVES = H // BANK
 UNIT_TILES = 4
 UNIT_ROWS = UNIT_TILES * P
 UNITS = B // UNIT_ROWS
+N_TILES = H // P
+BANK_TILES = BANK // P
 
 FLOPS = 2 * L * B * H * H
 
@@ -38,15 +40,11 @@ def tile_advancedliquidneuralnetwork_pa_kernel(tc, h, W_liq, b_liq, g_liq, beta_
         stage = ctx.enter_context(tc.tile_pool(name="stage", bufs=3))
         keep = ctx.enter_context(tc.tile_pool(name="keep", bufs=1))
         work = ctx.enter_context(tc.tile_pool(name="work", bufs=4))
-        acc_pool = ctx.enter_context(tc.tile_pool(name="acc", bufs=6))
+        z_pool = ctx.enter_context(tc.tile_pool(name="z", bufs=2 * UNIT_TILES))
+        acc_pool = ctx.enter_context(tc.tile_pool(name="acc", bufs=1))
+        out_pool = ctx.enter_context(tc.tile_pool(name="result", bufs=2))
         stats = ctx.enter_context(tc.tile_pool(name="stats", bufs=8))
         psum = ctx.enter_context(tc.psum_pool(name="psum", bufs=4))
-
-        rows = const.tile([P, H], BF16)
-        nc.vector.memset(rows[:].bitcast(I32), 0)
-        nc.scalar.dma_start(out=rows[0:L, :], in_=b_liq)
-        nc.scalar.dma_start(out=rows[L : 2 * L, :], in_=g_liq)
-        nc.scalar.dma_start(out=rows[2 * L : 3 * L, :], in_=beta_liq)
 
         def load_unit(name, dram_rows):
             raw = raw_pool.tile([P, UNIT_TILES, H], BF16, name=name)
@@ -59,6 +57,11 @@ def tile_advancedliquidneuralnetwork_pa_kernel(tc, h, W_liq, b_liq, g_liq, beta_
         h_raw = [None] * UNITS
         w_raw = {}
         h_raw[0] = load_unit("h_raw0", h[unit_rows(0), :])
+        rows = const.tile([P, H], BF16)
+        nc.vector.memset(rows[:].bitcast(I32), 0)
+        nc.sync.dma_start(out=rows[0:L, :], in_=b_liq)
+        nc.sync.dma_start(out=rows[L : 2 * L, :], in_=g_liq)
+        nc.sync.dma_start(out=rows[2 * L : 3 * L, :], in_=beta_liq)
         for l in range(L):
             for u in range(UNITS):
                 w_raw[(l, u)] = load_unit("w_raw%d_%d" % (l, u), W_liq[l, unit_rows(u), :])
@@ -73,29 +76,6 @@ def tile_advancedliquidneuralnetwork_pa_kernel(tc, h, W_liq, b_liq, g_liq, beta_
         warm = const.tile([P, 1], F32)
         nc.scalar.activation(out=warm[:], in_=eps[:], func=ACT.Sqrt)
 
-        def spread_rows(dest, picked):
-            for half in range(HALVES):
-                cols = slice(half * BANK, (half + 1) * BANK)
-                spread = psum.tile([P, BANK], F32, tag="t")
-                for r in picked:
-                    nc.tensor.matmul(
-                        out=spread[:],
-                        lhsT=ident_bf16[:, r : r + 1].to_broadcast([P, P]),
-                        rhs=rows[:, cols],
-                        start=(r == picked[0]),
-                        stop=(r == picked[-1]),
-                    )
-                nc.scalar.copy(out=dest[:, cols], in_=spread[:])
-
-        bias_bc = const.tile([P, L, H], BF16)
-        gain_bc = const.tile([P, L, H], BF16)
-        shift_bc = const.tile([P, H], F32)
-        for l in range(L):
-            spread_rows(bias_bc[:, l, :], [l])
-        for l in range(L):
-            spread_rows(gain_bc[:, l, :], [L + l])
-        spread_rows(shift_bc, [2 * L + l for l in range(L)])
-
         h_codes = keep.tile([P, PASSES, B], U32, align_bytes=64)
         h_scales = keep.tile([P, PASSES, B], U8, align_bytes=64)
         w_codes = keep.tile([P, L, PASSES, H], U32, align_bytes=64)
@@ -108,10 +88,14 @@ def tile_advancedliquidneuralnetwork_pa_kernel(tc, h, W_liq, b_liq, g_liq, beta_
                 raw_words = raw[:, j, :].bitcast(F32)
                 flipped = psum.tile([P, PASSES, 2, P], F32, tag="t")
                 for c in range(PASSES):
-                    for u in range(2):
-                        first = (2 * c + u) * P
-                        nc.tensor.transpose(flipped[:, c, u, :], raw_words[:, first : first + P], ident_f32[:])
-                nc.scalar.copy(out=grouped_words[:, :, j, :, :], in_=flipped[:].rearrange("p c u r -> p c r u"))
+                    for w in range(2):
+                        first = (2 * c + w) * P
+                        nc.tensor.transpose(flipped[:, c, w, :], raw_words[:, first : first + P], ident_f32[:])
+                side_by_side = flipped[:].rearrange("p c w r -> p c r w")
+                if j % 2 == 0:
+                    nc.scalar.copy(out=grouped_words[:, :, j, :, :], in_=side_by_side)
+                else:
+                    nc.vector.tensor_copy(out=grouped_words[:, :, j, :, :], in_=side_by_side)
             for c in range(PASSES):
                 nc.vector.quantize_mx(
                     out=codes[:, c, :].bitcast(FP8X4),
@@ -126,7 +110,27 @@ def tile_advancedliquidneuralnetwork_pa_kernel(tc, h, W_liq, b_liq, g_liq, beta_
             for u in range(UNITS):
                 quantise_unit(w_raw[(l, u)], w_codes[:, l, :, unit_rows(u)], w_scales[:, l, :, unit_rows(u)])
 
-        def branch(l, u, j, acc):
+        quantise_h(0)
+
+        bias_bc = const.tile([P, L, H], BF16)
+        for l in range(L):
+            for half in range(HALVES):
+                cols = slice(half * BANK, (half + 1) * BANK)
+                spread = psum.tile([P, BANK], F32, tag="t")
+                nc.tensor.matmul(
+                    out=spread[:], lhsT=ident_bf16[:, l : l + 1].to_broadcast([P, P]), rhs=rows[:, cols],
+                    start=True, stop=True,
+                )
+                nc.scalar.copy(out=bias_bc[:, l, cols], in_=spread[:])
+        rows_T = psum.tile([P, N_TILES, P], BF16, tag="t")
+        for t in range(N_TILES):
+            nc.tensor.transpose(rows_T[:, t, :], rows[:, t * P : (t + 1) * P], ident_bf16[:])
+        params_T = const.tile([P, N_TILES, 3 * L], F32)
+        nc.vector.tensor_copy(out=params_T[:], in_=rows_T[:, :, 0 : 3 * L])
+        shift_T = const.tile([P, N_TILES], F32)
+        nc.vector.tensor_reduce(out=shift_T[:], in_=params_T[:, :, 2 * L : 3 * L], axis=mybir.AxisListType.X, op=ADD)
+
+        def normalised_branch(l, u, j):
             tile_cols = slice((u * UNIT_TILES + j) * P, (u * UNIT_TILES + j + 1) * P)
             resid = work.tile([P, H], F32)
             nc.gpsimd.tensor_tensor(out=resid[:], in0=h_raw[u][:, j, :], in1=bias_bc[:, l, :], op=ADD)
@@ -153,31 +157,68 @@ def tile_advancedliquidneuralnetwork_pa_kernel(tc, h, W_liq, b_liq, g_liq, beta_
             nc.vector.tensor_scalar(
                 out=neg_mean[:], in0=row_sum[:, 0:1], scalar1=row_sum[:, 1:2], scalar2=-1.0 / H, op0=ADD, op1=MULT
             )
-            squares = work.tile([P, H], F32, bufs=2)
+            z = z_pool.tile([P, H], F32)
             sum_sq = stats.tile([P, 1], F32)
-            nc.scalar.activation(out=squares[:], in_=pre[:], func=ACT.Square, bias=neg_mean[:], scale=1.0, accum_out=sum_sq[:])
+            nc.scalar.activation(out=z[:], in_=pre[:], func=ACT.Square, bias=neg_mean[:], scale=1.0, accum_out=sum_sq[:])
             std = stats.tile([P, 1], F32)
             nc.scalar.activation(out=std[:], in_=sum_sq[:], func=ACT.Sqrt, bias=eps[:], scale=1.0 / H)
             rstd = stats.tile([P, 1], F32)
             nc.vector.reciprocal(rstd[:], std[:])
-            nc.vector.scalar_tensor_tensor(
-                out=pre[:], in0=pre[:], scalar=neg_mean[:], in1=gain_bc[:, l, :], op0=ADD, op1=MULT
-            )
-            nc.vector.scalar_tensor_tensor(
-                out=acc[:], in0=pre[:], scalar=rstd[:], in1=(shift_bc[:] if l == 0 else acc[:]), op0=MULT, op1=ADD
-            )
+            offset = stats.tile([P, 1], F32)
+            nc.vector.tensor_mul(offset[:], neg_mean[:], rstd[:])
+            nc.scalar.activation(out=z[:], in_=pre[:], func=ACT.Identity, bias=offset[:], scale=rstd[:])
+            return z
 
-        quantise_h(0)
+        def add_branch(l, zs, acc_T):
+            for t in range(N_TILES):
+                z_T = psum.tile([P, UNIT_TILES, P], F32, tag="t")
+                for j in range(UNIT_TILES):
+                    nc.tensor.transpose(z_T[:, j, :], zs[j][:, t * P : (t + 1) * P], ident_f32[:])
+                z_T_cols = z_T[:].rearrange("p j r -> p (j r)")
+                gain = params_T[:, t, L + l : L + l + 1]
+                if l == 0:
+                    nc.scalar.activation(
+                        out=acc_T[:, t, :], in_=z_T_cols, func=ACT.Identity, bias=shift_T[:, t : t + 1], scale=gain
+                    )
+                else:
+                    nc.vector.scalar_tensor_tensor(
+                        out=acc_T[:, t, :], in0=z_T_cols, scalar=gain, in1=acc_T[:, t, :], op0=MULT, op1=ADD
+                    )
+
+        def store_unit(u, acc_T):
+            for j in range(UNIT_TILES):
+                result = out_pool.tile([P, H], F32)
+                for half in range(HALVES):
+                    rows_back = psum.tile([P, BANK_TILES, P], F32, tag="t")
+                    for t in range(BANK_TILES):
+                        nc.tensor.transpose(
+                            rows_back[:, t, :], acc_T[:, half * BANK_TILES + t, j * P : (j + 1) * P], ident_f32[:]
+                        )
+                    nc.vector.tensor_copy(
+                        out=result[:, half * BANK : (half + 1) * BANK], in_=rows_back[:].rearrange("p t n -> p (t n)")
+                    )
+                first = (u * UNIT_TILES + j) * P
+                nc.sync.dma_start(out=out[first : first + P, :], in_=result[:])
+
+        acc_Ts = {}
+
+        def finish(u, l, zs):
+            if l == 0:
+                acc_Ts[u] = acc_pool.tile([P, N_TILES, UNIT_ROWS], F32, name="acc_T")
+            add_branch(l, zs, acc_Ts[u])
+            if l == L - 1:
+                store_unit(u, acc_Ts[u])
+
         quantise_w(0)
+        waiting = None
         for u in range(UNITS):
-            accs = [acc_pool.tile([P, H], F32, name="acc") for j in range(UNIT_TILES)]
             for l in range(L):
                 if u == 0 and l + 1 < L:
                     quantise_w(l + 1)
                 if u + 1 < UNITS and l == L - 1:
                     quantise_h(u + 1)
-                for j in range(UNIT_TILES):
-                    branch(l, u, j, accs[j])
-            for j in range(UNIT_TILES):
-                first = (u * UNIT_TILES + j) * P
-                nc.sync.dma_start(out=out[first : first + P, :], in_=accs[j][:])
+                zs = [normalised_branch(l, u, j) for j in range(UNIT_TILES)]
+                if waiting is not None:
+                    finish(*waiting)
+                waiting = (u, l, zs)
+        finish(*waiting)

@@ -133,7 +133,8 @@ def tile_advancedliquidneuralnetwork_pa_kernel(tc, h, W_liq, b_liq, g_liq, beta_
         def normalised_branch(l, u, j):
             tile_cols = slice((u * UNIT_TILES + j) * P, (u * UNIT_TILES + j + 1) * P)
             resid = work.tile([P, H], F32)
-            nc.gpsimd.tensor_tensor(out=resid[:], in0=h_raw[u][:, j, :], in1=bias_bc[:, l, :], op=ADD)
+            adder = nc.vector if l == 0 else nc.gpsimd
+            adder.tensor_tensor(out=resid[:], in0=h_raw[u][:, j, :], in1=bias_bc[:, l, :], op=ADD)
             pre = work.tile([P, H], F32)
             row_sum = stats.tile([P, HALVES], F32)
             for half in range(HALVES):

@@ -46,8 +46,8 @@ def tile_advancedliquidneuralnetwork_pa_kernel(tc, h, W_liq, b_liq, g_liq, beta_
         stats = ctx.enter_context(tc.tile_pool(name="stats", bufs=8))
         psum = ctx.enter_context(tc.psum_pool(name="psum", bufs=4))
 
-        def load_unit(name, dram_rows):
-            raw = raw_pool.tile([P, UNIT_TILES, H], BF16, name=name)
+        def load_unit(name, slots, dram_rows):
+            raw = raw_pool.tile([P, UNIT_TILES, H], BF16, name=name, bufs=slots)
             nc.sync.dma_start(out=raw[:], in_=dram_rows.rearrange("(j p) k -> p j k", p=P))
             return raw
 
@@ -56,7 +56,7 @@ def tile_advancedliquidneuralnetwork_pa_kernel(tc, h, W_liq, b_liq, g_liq, beta_
 
         h_raw = [None] * UNITS
         w_raw = {}
-        h_raw[0] = load_unit("h_raw0", h[unit_rows(0), :])
+        h_raw[0] = load_unit("h_raw", UNITS, h[unit_rows(0), :])
         rows = const.tile([P, H], BF16)
         nc.vector.memset(rows[:].bitcast(I32), 0)
         nc.sync.dma_start(out=rows[0:L, :], in_=b_liq)
@@ -64,8 +64,8 @@ def tile_advancedliquidneuralnetwork_pa_kernel(tc, h, W_liq, b_liq, g_liq, beta_
         nc.sync.dma_start(out=rows[2 * L : 3 * L, :], in_=beta_liq)
         for l in range(L):
             for u in range(UNITS):
-                w_raw[(l, u)] = load_unit("w_raw%d_%d" % (l, u), W_liq[l, unit_rows(u), :])
-        h_raw[1] = load_unit("h_raw1", h[unit_rows(1), :])
+                w_raw[(l, u)] = load_unit("w_raw", 4, W_liq[l, unit_rows(u), :])
+        h_raw[1] = load_unit("h_raw", UNITS, h[unit_rows(1), :])
 
         ident_f32 = const.tile([P, P], F32)
         make_identity(nc, ident_f32[:])
@@ -91,11 +91,7 @@ def tile_advancedliquidneuralnetwork_pa_kernel(tc, h, W_liq, b_liq, g_liq, beta_
                     for w in range(2):
                         first = (2 * c + w) * P
                         nc.tensor.transpose(flipped[:, c, w, :], raw_words[:, first : first + P], ident_f32[:])
-                side_by_side = flipped[:].rearrange("p c w r -> p c r w")
-                if j % 2 == 0:
-                    nc.scalar.copy(out=grouped_words[:, :, j, :, :], in_=side_by_side)
-                else:
-                    nc.vector.tensor_copy(out=grouped_words[:, :, j, :, :], in_=side_by_side)
+                nc.scalar.copy(out=grouped_words[:, :, j, :, :], in_=flipped[:].rearrange("p c w r -> p c r w"))
             for c in range(PASSES):
                 nc.vector.quantize_mx(
                     out=codes[:, c, :].bitcast(FP8X4),
@@ -132,9 +128,8 @@ def tile_advancedliquidneuralnetwork_pa_kernel(tc, h, W_liq, b_liq, g_liq, beta_
 
         def normalised_branch(l, u, j):
             tile_cols = slice((u * UNIT_TILES + j) * P, (u * UNIT_TILES + j + 1) * P)
-            resid = work.tile([P, H], F32)
-            adder = nc.vector if l == 0 else nc.gpsimd
-            adder.tensor_tensor(out=resid[:], in0=h_raw[u][:, j, :], in1=bias_bc[:, l, :], op=ADD)
+            resid = work.tile([P, H], F32, bufs=6)
+            nc.vector.tensor_tensor(out=resid[:], in0=h_raw[u][:, j, :], in1=bias_bc[:, l, :], op=ADD)
             pre = work.tile([P, H], F32)
             row_sum = stats.tile([P, HALVES], F32)
             for half in range(HALVES):
@@ -151,7 +146,7 @@ def tile_advancedliquidneuralnetwork_pa_kernel(tc, h, W_liq, b_liq, g_liq, beta_
                         stop=(c == PASSES - 1),
                     )
                 nc.vector.scalar_tensor_tensor(
-                    out=pre[:, cols], in0=product[:], scalar=0.0, in1=resid[:, cols],
+                    out=pre[:, cols], in0=resid[:, cols], scalar=0.0, in1=product[:],
                     op0=ADD, op1=ADD, accum_out=row_sum[:, half : half + 1],
                 )
             neg_mean = stats.tile([P, 1], F32)
@@ -165,9 +160,7 @@ def tile_advancedliquidneuralnetwork_pa_kernel(tc, h, W_liq, b_liq, g_liq, beta_
             nc.scalar.activation(out=std[:], in_=sum_sq[:], func=ACT.Sqrt, bias=eps[:], scale=1.0 / H)
             rstd = stats.tile([P, 1], F32)
             nc.vector.reciprocal(rstd[:], std[:])
-            offset = stats.tile([P, 1], F32)
-            nc.vector.tensor_mul(offset[:], neg_mean[:], rstd[:])
-            nc.scalar.activation(out=z[:], in_=pre[:], func=ACT.Identity, bias=offset[:], scale=rstd[:])
+            nc.gpsimd.tensor_scalar(out=z[:], in0=pre[:], scalar1=neg_mean[:], scalar2=rstd[:], op0=ADD, op1=MULT)
             return z
 
         def add_branch(l, zs, acc_T):
@@ -195,7 +188,7 @@ def tile_advancedliquidneuralnetwork_pa_kernel(tc, h, W_liq, b_liq, g_liq, beta_
                         nc.tensor.transpose(
                             rows_back[:, t, :], acc_T[:, half * BANK_TILES + t, j * P : (j + 1) * P], ident_f32[:]
                         )
-                    nc.vector.tensor_copy(
+                    nc.scalar.copy(
                         out=result[:, half * BANK : (half + 1) * BANK], in_=rows_back[:].rearrange("p t n -> p (t n)")
                     )
                 first = (u * UNIT_TILES + j) * P

@@ -28,6 +28,9 @@ UNIT_ROWS = UNIT_TILES * P
 UNITS = B // UNIT_ROWS
 N_TILES = H // P
 BANK_TILES = BANK // P
+STEPS = UNITS * L
+PAIR = 2
+W_RAW_SLOTS = 4
 
 FLOPS = 2 * L * B * H * H
 
@@ -39,12 +42,19 @@ def tile_advancedliquidneuralnetwork_pa_kernel(tc, h, W_liq, b_liq, g_liq, beta_
         raw_pool = ctx.enter_context(tc.tile_pool(name="raw", bufs=1))
         stage = ctx.enter_context(tc.tile_pool(name="stage", bufs=3))
         keep = ctx.enter_context(tc.tile_pool(name="keep", bufs=1))
-        work = ctx.enter_context(tc.tile_pool(name="work", bufs=4))
+        work = ctx.enter_context(tc.tile_pool(name="work", bufs=6))
         z_pool = ctx.enter_context(tc.tile_pool(name="z", bufs=2 * UNIT_TILES))
         acc_pool = ctx.enter_context(tc.tile_pool(name="acc", bufs=1))
         out_pool = ctx.enter_context(tc.tile_pool(name="result", bufs=2))
         stats = ctx.enter_context(tc.tile_pool(name="stats", bufs=8))
         psum = ctx.enter_context(tc.psum_pool(name="psum", bufs=4))
+        ctx.enter_context(tc.manual_schedule())
+
+        rows = const.tile([P, H], BF16)
+        nc.vector.memset(rows[:].bitcast(I32), 0)
+        nc.sync.dma_start(out=rows[0:L, :], in_=b_liq)
+        nc.sync.dma_start(out=rows[L : 2 * L, :], in_=g_liq)
+        nc.sync.dma_start(out=rows[2 * L : 3 * L, :], in_=beta_liq)
 
         def load_unit(name, slots, dram_rows):
             raw = raw_pool.tile([P, UNIT_TILES, H], BF16, name=name, bufs=slots)
@@ -57,56 +67,19 @@ def tile_advancedliquidneuralnetwork_pa_kernel(tc, h, W_liq, b_liq, g_liq, beta_
         h_raw = [None] * UNITS
         w_raw = {}
         h_raw[0] = load_unit("h_raw", UNITS, h[unit_rows(0), :])
-        rows = const.tile([P, H], BF16)
-        nc.vector.memset(rows[:].bitcast(I32), 0)
-        nc.sync.dma_start(out=rows[0:L, :], in_=b_liq)
-        nc.sync.dma_start(out=rows[L : 2 * L, :], in_=g_liq)
-        nc.sync.dma_start(out=rows[2 * L : 3 * L, :], in_=beta_liq)
         for l in range(L):
             for u in range(UNITS):
-                w_raw[(l, u)] = load_unit("w_raw", 4, W_liq[l, unit_rows(u), :])
+                w_raw[(l, u)] = load_unit("w_raw", W_RAW_SLOTS, W_liq[l, unit_rows(u), :])
         h_raw[1] = load_unit("h_raw", UNITS, h[unit_rows(1), :])
 
-        ident_f32 = const.tile([P, P], F32)
-        make_identity(nc, ident_f32[:])
         ident_bf16 = const.tile([P, P], BF16)
         make_identity(nc, ident_bf16[:])
+        ident_f32 = const.tile([P, P], F32)
+        make_identity(nc, ident_f32[:])
         eps = const.tile([P, 1], F32)
         nc.vector.memset(eps[:], LN_EPS)
         warm = const.tile([P, 1], F32)
         nc.scalar.activation(out=warm[:], in_=eps[:], func=ACT.Sqrt)
-
-        h_codes = keep.tile([P, PASSES, B], U32, align_bytes=64)
-        h_scales = keep.tile([P, PASSES, B], U8, align_bytes=64)
-        w_codes = keep.tile([P, L, PASSES, H], U32, align_bytes=64)
-        w_scales = keep.tile([P, L, PASSES, H], U8, align_bytes=64)
-
-        def quantise_unit(raw, codes, scales):
-            grouped = stage.tile([P, PASSES, UNIT_TILES, P, PACK], BF16, align_bytes=64)
-            grouped_words = grouped[:].bitcast(F32)
-            for j in range(UNIT_TILES):
-                raw_words = raw[:, j, :].bitcast(F32)
-                flipped = psum.tile([P, PASSES, 2, P], F32, tag="t")
-                for c in range(PASSES):
-                    for w in range(2):
-                        first = (2 * c + w) * P
-                        nc.tensor.transpose(flipped[:, c, w, :], raw_words[:, first : first + P], ident_f32[:])
-                nc.scalar.copy(out=grouped_words[:, :, j, :, :], in_=flipped[:].rearrange("p c w r -> p c r w"))
-            for c in range(PASSES):
-                nc.vector.quantize_mx(
-                    out=codes[:, c, :].bitcast(FP8X4),
-                    scales=scales[:, c, :],
-                    in_=grouped[:, c].rearrange("p j r t -> p (j r t)"),
-                )
-
-        def quantise_h(u):
-            quantise_unit(h_raw[u], h_codes[:, :, unit_rows(u)], h_scales[:, :, unit_rows(u)])
-
-        def quantise_w(l):
-            for u in range(UNITS):
-                quantise_unit(w_raw[(l, u)], w_codes[:, l, :, unit_rows(u)], w_scales[:, l, :, unit_rows(u)])
-
-        quantise_h(0)
 
         bias_bc = const.tile([P, L, H], BF16)
         for l in range(L):
@@ -117,7 +90,10 @@ def tile_advancedliquidneuralnetwork_pa_kernel(tc, h, W_liq, b_liq, g_liq, beta_
                     out=spread[:], lhsT=ident_bf16[:, l : l + 1].to_broadcast([P, P]), rhs=rows[:, cols],
                     start=True, stop=True,
                 )
-                nc.scalar.copy(out=bias_bc[:, l, cols], in_=spread[:])
+                if half == 0:
+                    nc.scalar.copy(out=bias_bc[:, l, cols], in_=spread[:])
+                else:
+                    nc.vector.tensor_copy(out=bias_bc[:, l, cols], in_=spread[:])
         rows_T = psum.tile([P, N_TILES, P], BF16, tag="t")
         for t in range(N_TILES):
             nc.tensor.transpose(rows_T[:, t, :], rows[:, t * P : (t + 1) * P], ident_bf16[:])
@@ -126,15 +102,58 @@ def tile_advancedliquidneuralnetwork_pa_kernel(tc, h, W_liq, b_liq, g_liq, beta_
         shift_T = const.tile([P, N_TILES], F32)
         nc.vector.tensor_reduce(out=shift_T[:], in_=params_T[:, :, 2 * L : 3 * L], axis=mybir.AxisListType.X, op=ADD)
 
-        def normalised_branch(l, u, j):
+        h_codes = keep.tile([P, PASSES, B], U32, align_bytes=64)
+        h_scales = keep.tile([P, PASSES, B], U8, align_bytes=64)
+        w_codes = keep.tile([P, L, PASSES, H], U32, align_bytes=64)
+        w_scales = keep.tile([P, L, PASSES, H], U8, align_bytes=64)
+
+        def operand(kind, l, u):
+            if kind == "h":
+                return h_raw[u], h_codes[:, :, unit_rows(u)], h_scales[:, :, unit_rows(u)]
+            return w_raw[(l, u)], w_codes[:, l, :, unit_rows(u)], w_scales[:, l, :, unit_rows(u)]
+
+        grouped_of = {}
+
+        def flip_operand(key):
+            raw = operand(*key)[0]
+            grouped = stage.tile([P, PASSES, UNIT_TILES, P, PACK], BF16, align_bytes=64)
+            grouped_of[key] = grouped
+            grouped_words = grouped[:].bitcast(F32)
+            flipped = []
+            for j in range(UNIT_TILES):
+                raw_words = raw[:, j, :].bitcast(F32)
+                flipped.append(psum.tile([P, PASSES, 2, P], F32, tag="t", name="flipped"))
+                for c in range(PASSES):
+                    for w in range(2):
+                        first = (2 * c + w) * P
+                        nc.tensor.transpose(flipped[j][:, c, w, :], raw_words[:, first : first + P], ident_f32[:])
+            for j in range(UNIT_TILES):
+                nc.scalar.copy(out=grouped_words[:, :, j, :, :], in_=flipped[j][:].rearrange("p c w r -> p c r w"))
+
+        def quantise_operand(key):
+            codes, scales = operand(*key)[1:]
+            for c in range(PASSES):
+                nc.vector.quantize_mx(
+                    out=codes[:, c, :].bitcast(FP8X4),
+                    scales=scales[:, c, :],
+                    in_=grouped_of[key][:, c].rearrange("p j r t -> p (j r t)"),
+                )
+
+        resid, products, pre, neg_mean, std, z, z_T, acc_T = {}, {}, {}, {}, {}, {}, {}, {}
+
+        def form_residual(k, j):
+            u, l = divmod(k, L)
+            resid[(k, j)] = work.tile([P, H], F32, name="resid")
+            nc.vector.tensor_tensor(out=resid[(k, j)][:], in0=h_raw[u][:, j, :], in1=bias_bc[:, l, :], op=ADD)
+
+        def multiply(k, j):
+            u, l = divmod(k, L)
             tile_cols = slice((u * UNIT_TILES + j) * P, (u * UNIT_TILES + j + 1) * P)
-            resid = work.tile([P, H], F32, bufs=6)
-            nc.vector.tensor_tensor(out=resid[:], in0=h_raw[u][:, j, :], in1=bias_bc[:, l, :], op=ADD)
-            pre = work.tile([P, H], F32)
-            row_sum = stats.tile([P, HALVES], F32)
+            products[(k, j)] = []
             for half in range(HALVES):
                 cols = slice(half * BANK, (half + 1) * BANK)
                 product = psum.tile([P, BANK], F32, tag="x")
+                products[(k, j)].append(product)
                 for c in range(PASSES):
                     nc.tensor.matmul_mx(
                         out=product[:],
@@ -145,48 +164,69 @@ def tile_advancedliquidneuralnetwork_pa_kernel(tc, h, W_liq, b_liq, g_liq, beta_
                         start=(c == 0),
                         stop=(c == PASSES - 1),
                     )
+
+        def add_residual(k, j):
+            pre[(k, j)] = work.tile([P, H], F32, name="pre")
+            row_sum = stats.tile([P, HALVES], F32)
+            for half in range(HALVES):
+                cols = slice(half * BANK, (half + 1) * BANK)
                 nc.vector.scalar_tensor_tensor(
-                    out=pre[:, cols], in0=resid[:, cols], scalar=0.0, in1=product[:],
+                    out=pre[(k, j)][:, cols], in0=resid[(k, j)][:, cols], scalar=0.0, in1=products[(k, j)][half][:],
                     op0=ADD, op1=ADD, accum_out=row_sum[:, half : half + 1],
                 )
-            neg_mean = stats.tile([P, 1], F32)
+            neg_mean[(k, j)] = stats.tile([P, 1], F32, name="neg_mean")
             nc.vector.tensor_scalar(
-                out=neg_mean[:], in0=row_sum[:, 0:1], scalar1=row_sum[:, 1:2], scalar2=-1.0 / H, op0=ADD, op1=MULT
+                out=neg_mean[(k, j)][:], in0=row_sum[:, 0:1], scalar1=row_sum[:, 1:2], scalar2=-1.0 / H,
+                op0=ADD, op1=MULT,
             )
-            z = z_pool.tile([P, H], F32)
-            sum_sq = stats.tile([P, 1], F32)
-            nc.scalar.activation(out=z[:], in_=pre[:], func=ACT.Square, bias=neg_mean[:], scale=1.0, accum_out=sum_sq[:])
-            std = stats.tile([P, 1], F32)
-            nc.scalar.activation(out=std[:], in_=sum_sq[:], func=ACT.Sqrt, bias=eps[:], scale=1.0 / H)
-            rstd = stats.tile([P, 1], F32)
-            nc.vector.reciprocal(rstd[:], std[:])
-            nc.gpsimd.tensor_scalar(out=z[:], in0=pre[:], scalar1=neg_mean[:], scalar2=rstd[:], op0=ADD, op1=MULT)
-            return z
 
-        def add_branch(l, zs, acc_T):
-            for t in range(N_TILES):
-                z_T = psum.tile([P, UNIT_TILES, P], F32, tag="t")
+        def sum_squares(k, j):
+            z[(k, j)] = z_pool.tile([P, H], F32, name="z")
+            sum_sq = stats.tile([P, 1], F32)
+            nc.scalar.activation(
+                out=z[(k, j)][:], in_=pre[(k, j)][:], func=ACT.Square, bias=neg_mean[(k, j)][:], scale=1.0,
+                accum_out=sum_sq[:],
+            )
+            std[(k, j)] = stats.tile([P, 1], F32, name="std")
+            nc.scalar.activation(out=std[(k, j)][:], in_=sum_sq[:], func=ACT.Sqrt, bias=eps[:], scale=1.0 / H)
+
+        def normalise(k, j):
+            rstd = stats.tile([P, 1], F32)
+            nc.vector.reciprocal(rstd[:], std[(k, j)][:])
+            nc.gpsimd.tensor_scalar(
+                out=z[(k, j)][:], in0=pre[(k, j)][:], scalar1=neg_mean[(k, j)][:], scalar2=rstd[:], op0=ADD, op1=MULT
+            )
+
+        def flip_branch(k, feature_tiles):
+            for t in feature_tiles:
+                z_T[(k, t)] = psum.tile([P, UNIT_TILES, P], F32, tag="t", name="z_T")
                 for j in range(UNIT_TILES):
-                    nc.tensor.transpose(z_T[:, j, :], zs[j][:, t * P : (t + 1) * P], ident_f32[:])
-                z_T_cols = z_T[:].rearrange("p j r -> p (j r)")
+                    nc.tensor.transpose(z_T[(k, t)][:, j, :], z[(k, j)][:, t * P : (t + 1) * P], ident_f32[:])
+
+        def add_branch(k, feature_tiles):
+            u, l = divmod(k, L)
+            if l == 0 and feature_tiles[0] == 0:
+                acc_T[u] = acc_pool.tile([P, N_TILES, UNIT_ROWS], F32, name="acc_T")
+            for t in feature_tiles:
+                z_T_cols = z_T[(k, t)][:].rearrange("p j r -> p (j r)")
                 gain = params_T[:, t, L + l : L + l + 1]
                 if l == 0:
                     nc.scalar.activation(
-                        out=acc_T[:, t, :], in_=z_T_cols, func=ACT.Identity, bias=shift_T[:, t : t + 1], scale=gain
+                        out=acc_T[u][:, t, :], in_=z_T_cols, func=ACT.Identity, bias=shift_T[:, t : t + 1], scale=gain
                     )
                 else:
                     nc.vector.scalar_tensor_tensor(
-                        out=acc_T[:, t, :], in0=z_T_cols, scalar=gain, in1=acc_T[:, t, :], op0=MULT, op1=ADD
+                        out=acc_T[u][:, t, :], in0=z_T_cols, scalar=gain, in1=acc_T[u][:, t, :], op0=MULT, op1=ADD
                     )
 
-        def store_unit(u, acc_T):
+        def store_unit(u):
             for j in range(UNIT_TILES):
                 result = out_pool.tile([P, H], F32)
                 for half in range(HALVES):
                     rows_back = psum.tile([P, BANK_TILES, P], F32, tag="t")
                     for t in range(BANK_TILES):
                         nc.tensor.transpose(
-                            rows_back[:, t, :], acc_T[:, half * BANK_TILES + t, j * P : (j + 1) * P], ident_f32[:]
+                            rows_back[:, t, :], acc_T[u][:, half * BANK_TILES + t, j * P : (j + 1) * P], ident_f32[:]
                         )
                     nc.scalar.copy(
                         out=result[:, half * BANK : (half + 1) * BANK], in_=rows_back[:].rearrange("p t n -> p (t n)")
@@ -194,25 +234,47 @@ def tile_advancedliquidneuralnetwork_pa_kernel(tc, h, W_liq, b_liq, g_liq, beta_
                 first = (u * UNIT_TILES + j) * P
                 nc.sync.dma_start(out=out[first : first + P, :], in_=result[:])
 
-        acc_Ts = {}
+        def operands_to_prepare(k):
+            u, l = divmod(k, L)
+            if u == 0 and l + 1 < L:
+                return [("w", l + 1, half) for half in range(UNITS)]
+            if l == L - 1 and u + 1 < UNITS:
+                return [("h", 0, u + 1)]
+            return []
 
-        def finish(u, l, zs):
-            if l == 0:
-                acc_Ts[u] = acc_pool.tile([P, N_TILES, UNIT_ROWS], F32, name="acc_T")
-            add_branch(l, zs, acc_Ts[u])
-            if l == L - 1:
-                store_unit(u, acc_Ts[u])
+        for key in [("h", 0, 0), ("w", 0, 0), ("w", 0, 1)]:
+            flip_operand(key)
+        for j in range(UNIT_TILES):
+            form_residual(0, j)
+        for key in [("h", 0, 0), ("w", 0, 0), ("w", 0, 1)]:
+            quantise_operand(key)
 
-        quantise_w(0)
-        waiting = None
-        for u in range(UNITS):
-            for l in range(L):
-                if u == 0 and l + 1 < L:
-                    quantise_w(l + 1)
-                if u + 1 < UNITS and l == L - 1:
-                    quantise_h(u + 1)
-                zs = [normalised_branch(l, u, j) for j in range(UNIT_TILES)]
-                if waiting is not None:
-                    finish(*waiting)
-                waiting = (u, l, zs)
-        finish(*waiting)
+        for k in range(STEPS + 1):
+            preparing = operands_to_prepare(k)
+            for part in range(UNIT_TILES // PAIR):
+                pair = range(part * PAIR, (part + 1) * PAIR)
+                feature_tiles = range(part * N_TILES // 2, (part + 1) * N_TILES // 2)
+                if part < len(preparing):
+                    flip_operand(preparing[part])
+                if k < STEPS:
+                    for j in pair:
+                        multiply(k, j)
+                if k > 0:
+                    flip_branch(k - 1, feature_tiles)
+                if k < STEPS:
+                    for j in pair:
+                        add_residual(k, j)
+                    for j in pair:
+                        sum_squares(k, j)
+                if k + 1 < STEPS:
+                    for j in pair:
+                        form_residual(k + 1, j)
+                if k < STEPS:
+                    for j in pair:
+                        normalise(k, j)
+                if k > 0:
+                    add_branch(k - 1, feature_tiles)
+                if part < len(preparing):
+                    quantise_operand(preparing[part])
+            if k > 0 and k % L == 0:
+                store_unit(k // L - 1)

from contextlib import ExitStack

import concourse.mybir as mybir
from concourse.masks import make_identity

F32 = mybir.dt.float32
BF16 = mybir.dt.bfloat16
U32 = mybir.dt.uint32
U8 = mybir.dt.uint8
I32 = mybir.dt.int32
FP8X4 = mybir.dt.float8_e4m3fn_x4
ADD = mybir.AluOpType.add
MULT = mybir.AluOpType.mult
ACT = mybir.ActivationFunctionType

P = 128
B = 1024
H = 1024
L = 3
LN_EPS = 1e-5
PACK = 4
K_PASS = P * PACK
PASSES = H // K_PASS
BANK = 512
HALVES = H // BANK
UNIT_TILES = 4
UNIT_ROWS = UNIT_TILES * P
UNITS = B // UNIT_ROWS
N_TILES = H // P
BANK_TILES = BANK // P
STEPS = UNITS * L
PAIR = 2
W_RAW_SLOTS = 4

FLOPS = 2 * L * B * H * H


def tile_advancedliquidneuralnetwork_pa_kernel(tc, h, W_liq, b_liq, g_liq, beta_liq, out):
    nc = tc.nc
    with ExitStack() as ctx:
        const = ctx.enter_context(tc.tile_pool(name="const", bufs=1))
        raw_pool = ctx.enter_context(tc.tile_pool(name="raw", bufs=1))
        stage = ctx.enter_context(tc.tile_pool(name="stage", bufs=3))
        keep = ctx.enter_context(tc.tile_pool(name="keep", bufs=1))
        work = ctx.enter_context(tc.tile_pool(name="work", bufs=6))
        z_pool = ctx.enter_context(tc.tile_pool(name="z", bufs=2 * UNIT_TILES))
        acc_pool = ctx.enter_context(tc.tile_pool(name="acc", bufs=1))
        out_pool = ctx.enter_context(tc.tile_pool(name="result", bufs=2))
        stats = ctx.enter_context(tc.tile_pool(name="stats", bufs=8))
        psum = ctx.enter_context(tc.psum_pool(name="psum", bufs=4))
        ctx.enter_context(tc.manual_schedule())

        rows = const.tile([P, H], BF16)
        nc.vector.memset(rows[:].bitcast(I32), 0)
        nc.sync.dma_start(out=rows[0:L, :], in_=b_liq)
        nc.sync.dma_start(out=rows[L : 2 * L, :], in_=g_liq)
        nc.sync.dma_start(out=rows[2 * L : 3 * L, :], in_=beta_liq)

        def load_unit(name, slots, dram_rows):
            raw = raw_pool.tile([P, UNIT_TILES, H], BF16, name=name, bufs=slots)
            nc.sync.dma_start(out=raw[:], in_=dram_rows.rearrange("(j p) k -> p j k", p=P))
            return raw

        def unit_rows(u):
            return slice(u * UNIT_ROWS, (u + 1) * UNIT_ROWS)

        h_raw = [None] * UNITS
        w_raw = {}
        h_raw[0] = load_unit("h_raw", UNITS, h[unit_rows(0), :])
        for l in range(L):
            for u in range(UNITS):
                w_raw[(l, u)] = load_unit("w_raw", W_RAW_SLOTS, W_liq[l, unit_rows(u), :])
        h_raw[1] = load_unit("h_raw", UNITS, h[unit_rows(1), :])

        ident_bf16 = const.tile([P, P], BF16)
        make_identity(nc, ident_bf16[:])
        ident_f32 = const.tile([P, P], F32)
        make_identity(nc, ident_f32[:])
        eps = const.tile([P, 1], F32)
        nc.vector.memset(eps[:], LN_EPS)
        warm = const.tile([P, 1], F32)
        nc.scalar.activation(out=warm[:], in_=eps[:], func=ACT.Sqrt)

        bias_bc = const.tile([P, L, H], BF16)
        for l in range(L):
            for half in range(HALVES):
                cols = slice(half * BANK, (half + 1) * BANK)
                spread = psum.tile([P, BANK], F32, tag="t")
                nc.tensor.matmul(
                    out=spread[:], lhsT=ident_bf16[:, l : l + 1].to_broadcast([P, P]), rhs=rows[:, cols],
                    start=True, stop=True,
                )
                if half == 0:
                    nc.scalar.copy(out=bias_bc[:, l, cols], in_=spread[:])
                else:
                    nc.vector.tensor_copy(out=bias_bc[:, l, cols], in_=spread[:])
        rows_T = psum.tile([P, N_TILES, P], BF16, tag="t")
        for t in range(N_TILES):
            nc.tensor.transpose(rows_T[:, t, :], rows[:, t * P : (t + 1) * P], ident_bf16[:])
        params_T = const.tile([P, N_TILES, 3 * L], F32)
        nc.vector.tensor_copy(out=params_T[:], in_=rows_T[:, :, 0 : 3 * L])
        shift_T = const.tile([P, N_TILES], F32)
        nc.vector.tensor_reduce(out=shift_T[:], in_=params_T[:, :, 2 * L : 3 * L], axis=mybir.AxisListType.X, op=ADD)

        h_codes = keep.tile([P, PASSES, B], U32, align_bytes=64)
        h_scales = keep.tile([P, PASSES, B], U8, align_bytes=64)
        w_codes = keep.tile([P, L, PASSES, H], U32, align_bytes=64)
        w_scales = keep.tile([P, L, PASSES, H], U8, align_bytes=64)

        def operand(kind, l, u):
            if kind == "h":
                return h_raw[u], h_codes[:, :, unit_rows(u)], h_scales[:, :, unit_rows(u)]
            return w_raw[(l, u)], w_codes[:, l, :, unit_rows(u)], w_scales[:, l, :, unit_rows(u)]

        grouped_of = {}

        def flip_operand(key):
            raw = operand(*key)[0]
            grouped = stage.tile([P, PASSES, UNIT_TILES, P, PACK], BF16, align_bytes=64)
            grouped_of[key] = grouped
            grouped_words = grouped[:].bitcast(F32)
            flipped = []
            for j in range(UNIT_TILES):
                raw_words = raw[:, j, :].bitcast(F32)
                flipped.append(psum.tile([P, PASSES, 2, P], F32, tag="t", name="flipped"))
                for c in range(PASSES):
                    for w in range(2):
                        first = (2 * c + w) * P
                        nc.tensor.transpose(flipped[j][:, c, w, :], raw_words[:, first : first + P], ident_f32[:])
            for j in range(UNIT_TILES):
                nc.scalar.copy(out=grouped_words[:, :, j, :, :], in_=flipped[j][:].rearrange("p c w r -> p c r w"))

        def quantise_operand(key):
            codes, scales = operand(*key)[1:]
            for c in range(PASSES):
                nc.vector.quantize_mx(
                    out=codes[:, c, :].bitcast(FP8X4),
                    scales=scales[:, c, :],
                    in_=grouped_of[key][:, c].rearrange("p j r t -> p (j r t)"),
                )

        resid, products, pre, neg_mean, std, z, z_T, acc_T = {}, {}, {}, {}, {}, {}, {}, {}

        def form_residual(k, j):
            u, l = divmod(k, L)
            resid[(k, j)] = work.tile([P, H], F32, name="resid")
            nc.vector.tensor_tensor(out=resid[(k, j)][:], in0=h_raw[u][:, j, :], in1=bias_bc[:, l, :], op=ADD)

        def multiply(k, j):
            u, l = divmod(k, L)
            tile_cols = slice((u * UNIT_TILES + j) * P, (u * UNIT_TILES + j + 1) * P)
            products[(k, j)] = []
            for half in range(HALVES):
                cols = slice(half * BANK, (half + 1) * BANK)
                product = psum.tile([P, BANK], F32, tag="x")
                products[(k, j)].append(product)
                for c in range(PASSES):
                    nc.tensor.matmul_mx(
                        out=product[:],
                        lhsT=h_codes[:, c, tile_cols].bitcast(FP8X4),
                        lhsT_scale=h_scales[:, c, tile_cols],
                        rhs=w_codes[:, l, c, cols].bitcast(FP8X4),
                        rhs_scale=w_scales[:, l, c, cols],
                        start=(c == 0),
                        stop=(c == PASSES - 1),
                    )

        def add_residual(k, j):
            pre[(k, j)] = work.tile([P, H], F32, name="pre")
            row_sum = stats.tile([P, HALVES], F32)
            for half in range(HALVES):
                cols = slice(half * BANK, (half + 1) * BANK)
                nc.vector.scalar_tensor_tensor(
                    out=pre[(k, j)][:, cols], in0=resid[(k, j)][:, cols], scalar=0.0, in1=products[(k, j)][half][:],
                    op0=ADD, op1=ADD, accum_out=row_sum[:, half : half + 1],
                )
            neg_mean[(k, j)] = stats.tile([P, 1], F32, name="neg_mean")
            nc.vector.tensor_scalar(
                out=neg_mean[(k, j)][:], in0=row_sum[:, 0:1], scalar1=row_sum[:, 1:2], scalar2=-1.0 / H,
                op0=ADD, op1=MULT,
            )

        def sum_squares(k, j):
            z[(k, j)] = z_pool.tile([P, H], F32, name="z")
            sum_sq = stats.tile([P, 1], F32)
            nc.scalar.activation(
                out=z[(k, j)][:], in_=pre[(k, j)][:], func=ACT.Square, bias=neg_mean[(k, j)][:], scale=1.0,
                accum_out=sum_sq[:],
            )
            std[(k, j)] = stats.tile([P, 1], F32, name="std")
            nc.scalar.activation(out=std[(k, j)][:], in_=sum_sq[:], func=ACT.Sqrt, bias=eps[:], scale=1.0 / H)

        def normalise(k, j):
            rstd = stats.tile([P, 1], F32)
            nc.vector.reciprocal(rstd[:], std[(k, j)][:])
            nc.gpsimd.tensor_scalar(
                out=z[(k, j)][:], in0=pre[(k, j)][:], scalar1=neg_mean[(k, j)][:], scalar2=rstd[:], op0=ADD, op1=MULT
            )

        def flip_branch(k, feature_tiles):
            for t in feature_tiles:
                z_T[(k, t)] = psum.tile([P, UNIT_TILES, P], F32, tag="t", name="z_T")
                for j in range(UNIT_TILES):
                    nc.tensor.transpose(z_T[(k, t)][:, j, :], z[(k, j)][:, t * P : (t + 1) * P], ident_f32[:])

        def add_branch(k, feature_tiles):
            u, l = divmod(k, L)
            if l == 0 and feature_tiles[0] == 0:
                acc_T[u] = acc_pool.tile([P, N_TILES, UNIT_ROWS], F32, name="acc_T")
            for t in feature_tiles:
                z_T_cols = z_T[(k, t)][:].rearrange("p j r -> p (j r)")
                gain = params_T[:, t, L + l : L + l + 1]
                if l == 0:
                    nc.scalar.activation(
                        out=acc_T[u][:, t, :], in_=z_T_cols, func=ACT.Identity, bias=shift_T[:, t : t + 1], scale=gain
                    )
                else:
                    nc.vector.scalar_tensor_tensor(
                        out=acc_T[u][:, t, :], in0=z_T_cols, scalar=gain, in1=acc_T[u][:, t, :], op0=MULT, op1=ADD
                    )

        def store_unit(u):
            for j in range(UNIT_TILES):
                result = out_pool.tile([P, H], F32)
                for half in range(HALVES):
                    rows_back = psum.tile([P, BANK_TILES, P], F32, tag="t")
                    for t in range(BANK_TILES):
                        nc.tensor.transpose(
                            rows_back[:, t, :], acc_T[u][:, half * BANK_TILES + t, j * P : (j + 1) * P], ident_f32[:]
                        )
                    nc.scalar.copy(
                        out=result[:, half * BANK : (half + 1) * BANK], in_=rows_back[:].rearrange("p t n -> p (t n)")
                    )
                first = (u * UNIT_TILES + j) * P
                nc.sync.dma_start(out=out[first : first + P, :], in_=result[:])

        def operands_to_prepare(k):
            u, l = divmod(k, L)
            if u == 0 and l + 1 < L:
                return [("w", l + 1, half) for half in range(UNITS)]
            if l == L - 1 and u + 1 < UNITS:
                return [("h", 0, u + 1)]
            return []

        for key in [("h", 0, 0), ("w", 0, 0), ("w", 0, 1)]:
            flip_operand(key)
        for j in range(UNIT_TILES):
            form_residual(0, j)
        for key in [("h", 0, 0), ("w", 0, 0), ("w", 0, 1)]:
            quantise_operand(key)

        for k in range(STEPS + 1):
            preparing = operands_to_prepare(k)
            for part in range(UNIT_TILES // PAIR):
                pair = range(part * PAIR, (part + 1) * PAIR)
                feature_tiles = range(part * N_TILES // 2, (part + 1) * N_TILES // 2)
                if part < len(preparing):
                    flip_operand(preparing[part])
                if k < STEPS:
                    for j in pair:
                        multiply(k, j)
                if k > 0:
                    flip_branch(k - 1, feature_tiles)
                if k < STEPS:
                    for j in pair:
                        add_residual(k, j)
                    for j in pair:
                        sum_squares(k, j)
                if k + 1 < STEPS:
                    for j in pair:
                        form_residual(k + 1, j)
                if k < STEPS:
                    for j in pair:
                        normalise(k, j)
                if k > 0:
                    add_branch(k - 1, feature_tiles)
                if part < len(preparing):
                    quantise_operand(preparing[part])
            if k > 0 and k % L == 0:
                store_unit(k // L - 1)
